import numpy as np
import ml_dtypes


def mxq(x, axis, fmt="e4m3"):
    dtype, down = {"e4m3": (ml_dtypes.float8_e4m3fn, 7), "e5m2": (ml_dtypes.float8_e5m2, 14)}[fmt]
    v = np.moveaxis(np.asarray(x, np.float32).astype(ml_dtypes.bfloat16).astype(np.float64), axis, -1)
    blocks = v.reshape(v.shape[:-1] + (-1, 32))
    amax = np.abs(blocks).max(-1, keepdims=True)
    byte = np.maximum(np.where(amax > 0, np.frexp(amax)[1] - 1 + 127, 0) - down, 1)
    scale = np.exp2(byte - 127.0)
    codes = (blocks / scale).astype(np.float32).astype(dtype).astype(np.float64)
    return np.moveaxis((codes * scale).reshape(v.shape), -1, axis)


WIDE = False


def mx_kscale(k):
    if not WIDE:
        return np.ones(k)
    levels = np.array([10, -10, 5, -5, 0])
    a = np.random.permutation(np.resize(levels, k // 512 * 4)).reshape(k // 512, 4)
    idx = np.arange(k)
    return np.exp2(a[idx // 512, idx % 128 // 32])


BF16 = ml_dtypes.bfloat16


def bf(x):
    return np.asarray(x, np.float32).astype(BF16)


def f64(x):
    return np.asarray(x).astype(np.float64)


B, S, D, H, DH = 4, 2048, 512, 2, 64
ROPE_BASE = 10000.0


def rope_tables():
    inv_freq = 1.0 / ROPE_BASE ** (np.arange(0, DH, 2) / DH)
    freqs = np.arange(S)[:, None] * inv_freq[None, :]
    emb = np.concatenate([freqs, freqs], axis=-1)
    return np.cos(emb), np.sin(emb)


def rotate_half(t):
    t1, t2 = t[..., : DH // 2], t[..., DH // 2 :]
    return np.concatenate([-t2, t1], axis=-1)


def setup_inputs():
    s = mx_kscale(D)
    c, sn = rope_tables()
    return {"x": bf(np.random.standard_normal((B, S, D)) * s),
            "Wq": bf(np.random.standard_normal((H * DH, D)) / np.sqrt(D) / s[None, :]),
            "Wk": bf(np.random.standard_normal((H * DH, D)) / np.sqrt(D) / s[None, :]),
            "rope_cos": bf(c), "rope_sin": bf(sn)}


def reference(x, Wq, Wk, rope_cos, rope_sin):
    xq = mxq(f64(x), 2, "e4m3")
    cos = f64(rope_cos)[None, None]
    sin = f64(rope_sin)[None, None]

    def proj(W):
        y = xq @ mxq(f64(W), 1, "e4m3").T
        return y.reshape(B, S, H, DH).transpose(0, 2, 1, 3)

    q, k = proj(Wq), proj(Wk)
    q_rot = q * cos + rotate_half(q) * sin
    k_rot = k * cos + rotate_half(k) * sin
    return q_rot, k_rot

@@ -1,0 +1,164 @@
+from contextlib import ExitStack
+
+import concourse.mybir as mybir
+from concourse.masks import make_identity
+
+F32 = mybir.dt.float32
+BF16 = mybir.dt.bfloat16
+U32 = mybir.dt.uint32
+U8 = mybir.dt.uint8
+FP8X4 = mybir.dt.float8_e4m3fn_x4
+MULT = mybir.AluOpType.mult
+ADD = mybir.AluOpType.add
+
+P = 128
+PACK = 4
+B, S, D = 4, 2048, 512
+HEADS, DH = 2, 64
+HALF = DH // 2
+GROUPS = 2 * HEADS
+FEATURES = GROUPS * DH
+SLOTS = S // P
+WORDS = D // 2
+CHUNK = 4
+CHUNKS_PER_BATCH = SLOTS // CHUNK
+N_CHUNKS = B * CHUNKS_PER_BATCH
+
+FLOPS = 2 * B * S * D * FEATURES
+
+
+def tile_attention_pa_t_kernel(tc, x, Wq, Wk, rope_cos, rope_sin, out_0, out_1):
+    nc = tc.nc
+    with ExitStack() as stack:
+        const = stack.enter_context(tc.tile_pool(name="const", bufs=1))
+        x_pool = stack.enter_context(tc.tile_pool(name="x", bufs=N_CHUNKS))
+        res_pool = stack.enter_context(tc.tile_pool(name="res", bufs=N_CHUNKS))
+        grouped_pool = stack.enter_context(tc.tile_pool(name="grouped", bufs=3))
+        codes_pool = stack.enter_context(tc.tile_pool(name="codes", bufs=2))
+        prod_pool = stack.enter_context(tc.tile_pool(name="prod", bufs=4))
+        xt_psum = stack.enter_context(tc.psum_pool(name="xt_psum", bufs=4))
+        y_psum = stack.enter_context(tc.psum_pool(name="y_psum", bufs=4))
+        stack.enter_context(tc.manual_schedule())
+
+        def chunk_place(c):
+            return c // CHUNKS_PER_BATCH, (c % CHUNKS_PER_BATCH) * CHUNK
+
+        def load_chunk(c):
+            b, t0 = chunk_place(c)
+            x_sb = x_pool.tile([P, CHUNK * D], BF16)
+            rows = x[b].rearrange("(p t) d -> p (t d)", t=SLOTS)
+            nc.sync.dma_start(out=x_sb[:], in_=rows[:, t0 * D : (t0 + CHUNK) * D])
+            return x_sb
+
+        def transpose_words(bank, rows_sb, first_word, column):
+            words = rows_sb[:].bitcast(F32)
+            for u in range(2):
+                nc.tensor.transpose(
+                    bank[:, u, column : column + P],
+                    words[:, first_word + u * P : first_word + (u + 1) * P],
+                    ident[:],
+                )
+
+        def transpose_chunk(x_sb):
+            grouped = grouped_pool.tile([P, CHUNK * P * PACK], BF16, align_bytes=64)
+            grouped_words = grouped[:].bitcast(F32).rearrange("p (n u) -> p n u", u=2)
+            for pair in range(CHUNK // 2):
+                bank = xt_psum.tile([P, 2, 2 * P], F32, tag="xt")
+                for i in range(2):
+                    transpose_words(bank, x_sb, (2 * pair + i) * WORDS, i * P)
+                nc.scalar.copy(
+                    out=grouped_words[:, pair * 2 * P : (pair + 1) * 2 * P, :],
+                    in_=bank[:].rearrange("p u n -> p n u"),
+                )
+            return grouped
+
+        def quantise_chunk(grouped):
+            x_codes = codes_pool.tile([P, CHUNK * P], U32, align_bytes=64)
+            x_scales = codes_pool.tile([P, CHUNK * P], U8, align_bytes=64)
+            nc.vector.quantize_mx(
+                out=x_codes[:].bitcast(FP8X4), scales=x_scales[:], in_=grouped[:]
+            )
+            return x_codes, x_scales
+
+        def project_tile(x_mx, i):
+            x_codes, x_scales = x_mx
+            tokens = slice(i * P, (i + 1) * P)
+            y = y_psum.tile([P, 2 * FEATURES], F32)
+            nc.tensor.matmul_mx(
+                out=y[:],
+                lhsT=x_codes[:, tokens].bitcast(FP8X4),
+                lhsT_scale=x_scales[:, tokens],
+                rhs=w_codes[:].bitcast(FP8X4),
+                rhs_scale=w_scales[:],
+                start=True,
+                stop=True,
+            )
+            return y
+
+        def rotate_tile(y, t, res, i):
+            products = prod_pool.tile([P, 2, GROUPS, DH], F32)
+            nc.vector.tensor_tensor(
+                out=products[:],
+                in0=y[:].rearrange("p (c g j) -> p c g j", c=2, g=GROUPS),
+                in1=tables[:, :, t, :].unsqueeze(2).to_broadcast([P, 2, GROUPS, DH]),
+                op=MULT,
+            )
+            nc.gpsimd.tensor_tensor(
+                out=res[:, :, i, :], in0=products[:, 0, :, :], in1=products[:, 1, :, :], op=ADD
+            )
+
+        def store_chunk(c, res):
+            b, t0 = chunk_place(c)
+            for o, out in enumerate((out_0, out_1)):
+                rows = out[b].rearrange("h (p t) j -> p h t j", t=SLOTS)
+                nc.sync.dma_start(
+                    out=rows[:, :, t0 : t0 + CHUNK, :], in_=res[:, o * HEADS : (o + 1) * HEADS, :, :]
+                )
+
+        ident = const.tile([P, P], F32)
+        make_identity(nc, ident[:])
+        wq_sb = const.tile([P, D], BF16)
+        nc.sync.dma_start(out=wq_sb[:], in_=Wq)
+        wk_sb = const.tile([P, D], BF16)
+        nc.sync.dma_start(out=wk_sb[:], in_=Wk)
+        x_tiles = [load_chunk(0), load_chunk(1)]
+        tables = const.tile([P, 2, SLOTS, DH], BF16)
+        nc.sync.dma_start(out=tables[:, 0, :, :], in_=rope_cos.rearrange("(p t) j -> p t j", t=SLOTS))
+        nc.sync.dma_start(out=tables[:, 1, :, :], in_=rope_sin.rearrange("(p t) j -> p t j", t=SLOTS))
+        for c in range(2, N_CHUNKS):
+            x_tiles.append(load_chunk(c))
+
+        w_bank = xt_psum.tile([P, 2, 2 * P], F32, tag="xt")
+        transpose_words(w_bank, wq_sb, 0, 0)
+        transpose_words(w_bank, wk_sb, 0, P)
+        w_grouped = const.tile([P, 2 * FEATURES * PACK], BF16, align_bytes=64)
+        w_words = w_grouped[:].bitcast(F32).rearrange("p (n u) -> p n u", u=2)
+        nc.vector.tensor_copy(out=w_words[:, 0:FEATURES, :], in_=w_bank[:].rearrange("p u n -> p n u"))
+        swapped = w_words[:, FEATURES : 2 * FEATURES, :].rearrange(
+            "p (g a j) u -> p g a j u", g=GROUPS, a=2
+        )
+        straight = w_bank[:].rearrange("p u (g a j) -> p g a j u", g=GROUPS, a=2)
+        for a in range(2):
+            nc.vector.tensor_copy(out=swapped[:, :, a, :, :], in_=straight[:, :, 1 - a, :, :])
+        w_codes = const.tile([P, 2 * FEATURES], U32, align_bytes=64)
+        w_scales = const.tile([P, 2 * FEATURES], U8, align_bytes=64)
+        nc.vector.quantize_mx(out=w_codes[:].bitcast(FP8X4), scales=w_scales[:], in_=w_grouped[:])
+
+        x_mx = quantise_chunk(transpose_chunk(x_tiles[0]))
+        nc.vector.tensor_scalar_mul(
+            out=tables[:, 1, :, 0:HALF], in0=tables[:, 1, :, 0:HALF], scalar1=-1.0
+        )
+        grouped_next = transpose_chunk(x_tiles[1])
+        y_tiles = [project_tile(x_mx, i) for i in range(CHUNK)]
+        for c in range(N_CHUNKS):
+            if c + 1 < N_CHUNKS:
+                x_mx = quantise_chunk(grouped_next)
+            if c + 2 < N_CHUNKS:
+                grouped_next = transpose_chunk(x_tiles[c + 2])
+            res = res_pool.tile([P, GROUPS, CHUNK, DH], F32)
+            first_slot = chunk_place(c)[1]
+            for i in range(CHUNK):
+                rotate_tile(y_tiles[i], first_slot + i, res, i)
+                if c + 1 < N_CHUNKS:
+                    y_tiles[i] = project_tile(x_mx, i)
+            store_chunk(c, res)

@@ -35,7 +35,7 @@ def tile_attention_pa_t_kernel(tc, x, Wq, Wk, rope_cos, rope_sin, out_0, out_1):
         res_pool = stack.enter_context(tc.tile_pool(name="res", bufs=N_CHUNKS))
         grouped_pool = stack.enter_context(tc.tile_pool(name="grouped", bufs=3))
         codes_pool = stack.enter_context(tc.tile_pool(name="codes", bufs=2))
-        prod_pool = stack.enter_context(tc.tile_pool(name="prod", bufs=4))
+        prod_pool = stack.enter_context(tc.tile_pool(name="prod", bufs=3))
         xt_psum = stack.enter_context(tc.psum_pool(name="xt_psum", bufs=4))
         y_psum = stack.enter_context(tc.psum_pool(name="y_psum", bufs=4))
         stack.enter_context(tc.manual_schedule())
@@ -95,16 +95,12 @@ def tile_attention_pa_t_kernel(tc, x, Wq, Wk, rope_cos, rope_sin, out_0, out_1):
             )
             return y
 
-        def rotate_tile(y, t, res, i):
-            products = prod_pool.tile([P, 2, GROUPS, DH], F32)
+        def multiply_tile(y, t, products, i):
             nc.vector.tensor_tensor(
-                out=products[:],
+                out=products[:, :, :, i, :],
                 in0=y[:].rearrange("p (c g j) -> p c g j", c=2, g=GROUPS),
                 in1=tables[:, :, t, :].unsqueeze(2).to_broadcast([P, 2, GROUPS, DH]),
                 op=MULT,
-            )
-            nc.gpsimd.tensor_tensor(
-                out=res[:, :, i, :], in0=products[:, 0, :, :], in1=products[:, 1, :, :], op=ADD
             )
 
         def store_chunk(c, res):
@@ -155,10 +151,15 @@ def tile_attention_pa_t_kernel(tc, x, Wq, Wk, rope_cos, rope_sin, out_0, out_1):
                 x_mx = quantise_chunk(grouped_next)
             if c + 2 < N_CHUNKS:
                 grouped_next = transpose_chunk(x_tiles[c + 2])
-            res = res_pool.tile([P, GROUPS, CHUNK, DH], F32)
+            products = prod_pool.tile([P, 2, GROUPS, CHUNK, DH], F32)
             first_slot = chunk_place(c)[1]
             for i in range(CHUNK):
-                rotate_tile(y_tiles[i], first_slot + i, res, i)
+                multiply_tile(y_tiles[i], first_slot + i, products, i)
                 if c + 1 < N_CHUNKS:
                     y_tiles[i] = project_tile(x_mx, i)
+            adder = nc.vector if c == N_CHUNKS - 1 else nc.gpsimd
+            res = res_pool.tile([P, GROUPS, CHUNK, DH], F32)
+            adder.tensor_tensor(
+                out=res[:], in0=products[:, 0, :, :, :], in1=products[:, 1, :, :, :], op=ADD
+            )
             store_chunk(c, res)

@@ -23,6 +23,7 @@ WORDS = D // 2
 CHUNK = 4
 CHUNKS_PER_BATCH = SLOTS // CHUNK
 N_CHUNKS = B * CHUNKS_PER_BATCH
+GPSIMD_GROUPS = 3
 
 FLOPS = 2 * B * S * D * FEATURES
 
@@ -157,9 +158,19 @@ def tile_attention_pa_t_kernel(tc, x, Wq, Wk, rope_cos, rope_sin, out_0, out_1):
                 multiply_tile(y_tiles[i], first_slot + i, products, i)
                 if c + 1 < N_CHUNKS:
                     y_tiles[i] = project_tile(x_mx, i)
-            adder = nc.vector if c == N_CHUNKS - 1 else nc.gpsimd
+            split = 0 if c == N_CHUNKS - 1 else GPSIMD_GROUPS
             res = res_pool.tile([P, GROUPS, CHUNK, DH], F32)
-            adder.tensor_tensor(
-                out=res[:], in0=products[:, 0, :, :, :], in1=products[:, 1, :, :, :], op=ADD
+            nc.vector.tensor_tensor(
+                out=res[:, split:GROUPS, :, :],
+                in0=products[:, 0, split:GROUPS, :, :],
+                in1=products[:, 1, split:GROUPS, :, :],
+                op=ADD,
             )
+            if split > 0:
+                nc.gpsimd.tensor_tensor(
+                    out=res[:, 0:split, :, :],
+                    in0=products[:, 0, 0:split, :, :],
+                    in1=products[:, 1, 0:split, :, :],
+                    op=ADD,
+                )
             store_chunk(c, res)

from contextlib import ExitStack

import concourse.mybir as mybir
from concourse.masks import make_identity

F32 = mybir.dt.float32
BF16 = mybir.dt.bfloat16
U32 = mybir.dt.uint32
U8 = mybir.dt.uint8
FP8X4 = mybir.dt.float8_e4m3fn_x4
MULT = mybir.AluOpType.mult
ADD = mybir.AluOpType.add

P = 128
PACK = 4
B, S, D = 4, 2048, 512
HEADS, DH = 2, 64
HALF = DH // 2
GROUPS = 2 * HEADS
FEATURES = GROUPS * DH
SLOTS = S // P
WORDS = D // 2
CHUNK = 4
CHUNKS_PER_BATCH = SLOTS // CHUNK
N_CHUNKS = B * CHUNKS_PER_BATCH
GPSIMD_GROUPS = 3

FLOPS = 2 * B * S * D * FEATURES


def tile_attention_pa_t_kernel(tc, x, Wq, Wk, rope_cos, rope_sin, out_0, out_1):
    nc = tc.nc
    with ExitStack() as stack:
        const = stack.enter_context(tc.tile_pool(name="const", bufs=1))
        x_pool = stack.enter_context(tc.tile_pool(name="x", bufs=N_CHUNKS))
        res_pool = stack.enter_context(tc.tile_pool(name="res", bufs=N_CHUNKS))
        grouped_pool = stack.enter_context(tc.tile_pool(name="grouped", bufs=3))
        codes_pool = stack.enter_context(tc.tile_pool(name="codes", bufs=2))
        prod_pool = stack.enter_context(tc.tile_pool(name="prod", bufs=3))
        xt_psum = stack.enter_context(tc.psum_pool(name="xt_psum", bufs=4))
        y_psum = stack.enter_context(tc.psum_pool(name="y_psum", bufs=4))
        stack.enter_context(tc.manual_schedule())

        def chunk_place(c):
            return c // CHUNKS_PER_BATCH, (c % CHUNKS_PER_BATCH) * CHUNK

        def load_chunk(c):
            b, t0 = chunk_place(c)
            x_sb = x_pool.tile([P, CHUNK * D], BF16)
            rows = x[b].rearrange("(p t) d -> p (t d)", t=SLOTS)
            nc.sync.dma_start(out=x_sb[:], in_=rows[:, t0 * D : (t0 + CHUNK) * D])
            return x_sb

        def transpose_words(bank, rows_sb, first_word, column):
            words = rows_sb[:].bitcast(F32)
            for u in range(2):
                nc.tensor.transpose(
                    bank[:, u, column : column + P],
                    words[:, first_word + u * P : first_word + (u + 1) * P],
                    ident[:],
                )

        def transpose_chunk(x_sb):
            grouped = grouped_pool.tile([P, CHUNK * P * PACK], BF16, align_bytes=64)
            grouped_words = grouped[:].bitcast(F32).rearrange("p (n u) -> p n u", u=2)
            for pair in range(CHUNK // 2):
                bank = xt_psum.tile([P, 2, 2 * P], F32, tag="xt")
                for i in range(2):
                    transpose_words(bank, x_sb, (2 * pair + i) * WORDS, i * P)
                nc.scalar.copy(
                    out=grouped_words[:, pair * 2 * P : (pair + 1) * 2 * P, :],
                    in_=bank[:].rearrange("p u n -> p n u"),
                )
            return grouped

        def quantise_chunk(grouped):
            x_codes = codes_pool.tile([P, CHUNK * P], U32, align_bytes=64)
            x_scales = codes_pool.tile([P, CHUNK * P], U8, align_bytes=64)
            nc.vector.quantize_mx(
                out=x_codes[:].bitcast(FP8X4), scales=x_scales[:], in_=grouped[:]
            )
            return x_codes, x_scales

        def project_tile(x_mx, i):
            x_codes, x_scales = x_mx
            tokens = slice(i * P, (i + 1) * P)
            y = y_psum.tile([P, 2 * FEATURES], F32)
            nc.tensor.matmul_mx(
                out=y[:],
                lhsT=x_codes[:, tokens].bitcast(FP8X4),
                lhsT_scale=x_scales[:, tokens],
                rhs=w_codes[:].bitcast(FP8X4),
                rhs_scale=w_scales[:],
                start=True,
                stop=True,
            )
            return y

        def multiply_tile(y, t, products, i):
            nc.vector.tensor_tensor(
                out=products[:, :, :, i, :],
                in0=y[:].rearrange("p (c g j) -> p c g j", c=2, g=GROUPS),
                in1=tables[:, :, t, :].unsqueeze(2).to_broadcast([P, 2, GROUPS, DH]),
                op=MULT,
            )

        def store_chunk(c, res):
            b, t0 = chunk_place(c)
            for o, out in enumerate((out_0, out_1)):
                rows = out[b].rearrange("h (p t) j -> p h t j", t=SLOTS)
                nc.sync.dma_start(
                    out=rows[:, :, t0 : t0 + CHUNK, :], in_=res[:, o * HEADS : (o + 1) * HEADS, :, :]
                )

        ident = const.tile([P, P], F32)
        make_identity(nc, ident[:])
        wq_sb = const.tile([P, D], BF16)
        nc.sync.dma_start(out=wq_sb[:], in_=Wq)
        wk_sb = const.tile([P, D], BF16)
        nc.sync.dma_start(out=wk_sb[:], in_=Wk)
        x_tiles = [load_chunk(0), load_chunk(1)]
        tables = const.tile([P, 2, SLOTS, DH], BF16)
        nc.sync.dma_start(out=tables[:, 0, :, :], in_=rope_cos.rearrange("(p t) j -> p t j", t=SLOTS))
        nc.sync.dma_start(out=tables[:, 1, :, :], in_=rope_sin.rearrange("(p t) j -> p t j", t=SLOTS))
        for c in range(2, N_CHUNKS):
            x_tiles.append(load_chunk(c))

        w_bank = xt_psum.tile([P, 2, 2 * P], F32, tag="xt")
        transpose_words(w_bank, wq_sb, 0, 0)
        transpose_words(w_bank, wk_sb, 0, P)
        w_grouped = const.tile([P, 2 * FEATURES * PACK], BF16, align_bytes=64)
        w_words = w_grouped[:].bitcast(F32).rearrange("p (n u) -> p n u", u=2)
        nc.vector.tensor_copy(out=w_words[:, 0:FEATURES, :], in_=w_bank[:].rearrange("p u n -> p n u"))
        swapped = w_words[:, FEATURES : 2 * FEATURES, :].rearrange(
            "p (g a j) u -> p g a j u", g=GROUPS, a=2
        )
        straight = w_bank[:].rearrange("p u (g a j) -> p g a j u", g=GROUPS, a=2)
        for a in range(2):
            nc.vector.tensor_copy(out=swapped[:, :, a, :, :], in_=straight[:, :, 1 - a, :, :])
        w_codes = const.tile([P, 2 * FEATURES], U32, align_bytes=64)
        w_scales = const.tile([P, 2 * FEATURES], U8, align_bytes=64)
        nc.vector.quantize_mx(out=w_codes[:].bitcast(FP8X4), scales=w_scales[:], in_=w_grouped[:])

        x_mx = quantise_chunk(transpose_chunk(x_tiles[0]))
        nc.vector.tensor_scalar_mul(
            out=tables[:, 1, :, 0:HALF], in0=tables[:, 1, :, 0:HALF], scalar1=-1.0
        )
        grouped_next = transpose_chunk(x_tiles[1])
        y_tiles = [project_tile(x_mx, i) for i in range(CHUNK)]
        for c in range(N_CHUNKS):
            if c + 1 < N_CHUNKS:
                x_mx = quantise_chunk(grouped_next)
            if c + 2 < N_CHUNKS:
                grouped_next = transpose_chunk(x_tiles[c + 2])
            products = prod_pool.tile([P, 2, GROUPS, CHUNK, DH], F32)
            first_slot = chunk_place(c)[1]
            for i in range(CHUNK):
                multiply_tile(y_tiles[i], first_slot + i, products, i)
                if c + 1 < N_CHUNKS:
                    y_tiles[i] = project_tile(x_mx, i)
            split = 0 if c == N_CHUNKS - 1 else GPSIMD_GROUPS
            res = res_pool.tile([P, GROUPS, CHUNK, DH], F32)
            nc.vector.tensor_tensor(
                out=res[:, split:GROUPS, :, :],
                in0=products[:, 0, split:GROUPS, :, :],
                in1=products[:, 1, split:GROUPS, :, :],
                op=ADD,
            )
            if split > 0:
                nc.gpsimd.tensor_tensor(
                    out=res[:, 0:split, :, :],
                    in0=products[:, 0, 0:split, :, :],
                    in1=products[:, 1, 0:split, :, :],
                    op=ADD,
                )
            store_chunk(c, res)
